import numpy as np
import ml_dtypes


def mxq(x, axis, fmt="e4m3"):
    dtype, down = {"e4m3": (ml_dtypes.float8_e4m3fn, 7), "e5m2": (ml_dtypes.float8_e5m2, 14)}[fmt]
    v = np.moveaxis(np.asarray(x, np.float32).astype(ml_dtypes.bfloat16).astype(np.float64), axis, -1)
    blocks = v.reshape(v.shape[:-1] + (-1, 32))
    amax = np.abs(blocks).max(-1, keepdims=True)
    byte = np.maximum(np.where(amax > 0, np.frexp(amax)[1] - 1 + 127, 0) - down, 1)
    scale = np.exp2(byte - 127.0)
    codes = (blocks / scale).astype(np.float32).astype(dtype).astype(np.float64)
    return np.moveaxis((codes * scale).reshape(v.shape), -1, axis)


WIDE = False


def mx_kscale(k):
    if not WIDE:
        return np.ones(k)
    levels = np.array([10, -10, 5, -5, 0])
    a = np.random.permutation(np.resize(levels, k // 512 * 4)).reshape(k // 512, 4)
    idx = np.arange(k)
    return np.exp2(a[idx // 512, idx % 128 // 32])


BF16 = ml_dtypes.bfloat16


def bf(x):
    return np.asarray(x, np.float32).astype(BF16)


def f64(x):
    return np.asarray(x).astype(np.float64)


B, S, D, DFF, R = 4, 128, 1024, 4096, 512


def erf(z):
    z2 = z * z
    acc = np.zeros_like(z)
    for c in (np.arange(13) + 0.5) ** 2 * 0.25:
        acc += np.exp(-c) / (c + z2)
    return np.tanh(2.0 * np.pi * z) - z * np.exp(-z2) / np.pi * acc


def gelu_erf(v):
    return 0.5 * v * (1.0 + erf(v / np.sqrt(2.0)))


def setup_inputs():
    s, r = mx_kscale(D), mx_kscale(R)
    return {"x": bf(np.random.standard_normal((B, S, D)) * s),
            "c_fc_U": bf(np.random.standard_normal((D, R)) * 2.0 / np.sqrt(D) / s[:, None]),
            "c_fc_S": bf(np.random.uniform(size=R) * r),
            "c_fc_V": bf(np.random.standard_normal((DFF, R)) / np.sqrt(R) / r[None, :]),
            "c_fc_bias": bf(np.random.standard_normal(DFF) * 0.3)}


def reference(x, c_fc_U, c_fc_S, c_fc_V, c_fc_bias):
    us = f64(c_fc_U) * f64(c_fc_S)[None, :]
    w = mxq(us, 1, "e4m3") @ mxq(f64(c_fc_V), 1, "e4m3").T
    h = (mxq(f64(x), 2, "e4m3") @ mxq(w, 0, "e4m3")) + f64(c_fc_bias)
    return gelu_erf(h)

@@ -1,0 +1,213 @@
+from contextlib import ExitStack
+
+import concourse.mybir as mybir
+from concourse.masks import make_identity
+
+F32 = mybir.dt.float32
+BF16 = mybir.dt.bfloat16
+U32 = mybir.dt.uint32
+U8 = mybir.dt.uint8
+FP8X4 = mybir.dt.float8_e4m3fn_x4
+ALU = mybir.AluOpType
+ACT = mybir.ActivationFunctionType
+
+P = 128
+PACK = 4
+BATCH, SEQ, D, DFF, R = 4, 128, 1024, 4096, 512
+BANK = 512
+CHUNK = 512
+N_CHUNKS = DFF // CHUNK
+D_PASSES = D // (P * PACK)
+SLOTS_PER_CHUNK = 4
+W_SLOTS = N_CHUNKS * SLOTS_PER_CHUNK
+LAG = 5
+X_SLOT = 2
+VECTOR_W_SLOT = 2
+
+FLOPS = 2 * D * DFF * R + 2 * BATCH * SEQ * D * DFF
+
+
+def tile_hybridsuperlayer_pa_kernel(tc, x, c_fc_U, c_fc_S, c_fc_V, c_fc_bias, out):
+    nc = tc.nc
+    with ExitStack() as ctx:
+        resident = ctx.enter_context(tc.tile_pool(name="resident", bufs=1))
+        staging = ctx.enter_context(tc.tile_pool(name="staging", bufs=3))
+        w_pool = ctx.enter_context(tc.tile_pool(name="w_pool", bufs=3))
+        h_pool = ctx.enter_context(tc.tile_pool(name="h_pool", bufs=6))
+        psum = ctx.enter_context(tc.psum_pool(name="psum", bufs=8))
+
+        s_grid = resident.tile([P, 2, 2], BF16, name="s_grid")
+        nc.sync.dma_start(out=s_grid[:], in_=c_fc_S.rearrange("(u p e) -> p u e", u=2, p=P, e=2))
+
+        u_rows = c_fc_U.rearrange("(g u m e) r -> g m u e r", g=D_PASSES, u=2, m=P, e=2)
+        u_raw = [resident.tile([P, PACK * R], BF16, name="u_raw%d" % g) for g in range(D_PASSES)]
+        v_rows = c_fc_V.rearrange("(c a p) r -> c p a r", c=N_CHUNKS, a=CHUNK // P, p=P)
+        v_raw = [resident.tile([P, CHUNK // P * R], BF16, name="v_raw%d" % c) for c in range(N_CHUNKS)]
+        x_raw = [resident.tile([P, 2 * D], BF16, name="x_raw%d" % pair) for pair in range(BATCH // 2)]
+        bias_all = resident.tile([P, DFF], BF16, name="bias_all")
+
+        def load_u(g):
+            nc.sync.dma_start(
+                out=u_raw[g][:].rearrange("m (u e r) -> m u e r", u=2, e=2), in_=u_rows[g]
+            )
+
+        def load_v(c):
+            nc.sync.dma_start(out=v_raw[c][:].rearrange("p (a r) -> p a r", r=R), in_=v_rows[c])
+
+        load_u(0)
+        load_v(0)
+        load_u(1)
+        load_v(1)
+        for pair in range(BATCH // 2):
+            nc.sync.dma_start(
+                out=x_raw[pair][:].rearrange("s (j d) -> s j d", j=2),
+                in_=x[2 * pair : 2 * pair + 2].rearrange("j s d -> s j d"),
+            )
+        load_v(2)
+        nc.sync.dma_start(out=bias_all[:], in_=c_fc_bias.partition_broadcast(P))
+        for c in range(3, N_CHUNKS):
+            load_v(c)
+
+        identity = resident.tile([P, P], F32, name="identity")
+        make_identity(nc, identity[:])
+
+        table_warmer = resident.tile([P, 1], F32, name="table_warmer")
+        nc.vector.memset(table_warmer[:], 0.0)
+        nc.scalar.activation(out=table_warmer[:], in_=table_warmer[:], func=ACT.Gelu)
+
+        us_codes = [resident.tile([P, BANK], U32, name="us_codes%d" % g, align_bytes=64) for g in range(D_PASSES)]
+        us_scales = [resident.tile([P, BANK], U8, name="us_scales%d" % g, align_bytes=64) for g in range(D_PASSES)]
+        x_codes = [resident.tile([P, BANK], U32, name="x_codes%d" % g, align_bytes=64) for g in range(D_PASSES)]
+        x_scales = [resident.tile([P, BANK], U8, name="x_scales%d" % g, align_bytes=64) for g in range(D_PASSES)]
+        v_codes = [resident.tile([P, CHUNK], U32, name="v_codes%d" % c, align_bytes=64) for c in range(N_CHUNKS)]
+        v_scales = [resident.tile([P, CHUNK], U8, name="v_scales%d" % c, align_bytes=64) for c in range(N_CHUNKS)]
+        w_codes = {}
+        w_scales = {}
+
+        waiting = {}
+
+        def quantise_later(slot, grouped, codes, scales):
+            waiting[slot] = waiting.get(slot, []) + [(grouped, codes, scales)]
+
+        def quantise_what_waits(slot):
+            for grouped, codes, scales in waiting.get(slot, []):
+                nc.vector.quantize_mx(out=codes.bitcast(FP8X4), scales=scales, in_=grouped)
+
+        def transpose_words(row_tiles):
+            bank = psum.tile([P, BANK], F32, name="bank", tag="bank")
+            for j in range(2):
+                for u in range(2):
+                    nc.tensor.transpose(
+                        bank[:, 256 * u + P * j : 256 * u + P * j + P],
+                        row_tiles[j][:, P * u : P * u + P],
+                        identity[:],
+                    )
+            return bank
+
+        def copy_words_out(copy, grouped_half, bank):
+            copy(
+                out=grouped_half.bitcast(F32).rearrange("p (c u) -> p c u", u=2),
+                in_=bank[:].rearrange("p (u c) -> p c u", u=2),
+            )
+
+        def prepare_us(slot, g):
+            words = u_raw[g][:].bitcast(F32)
+            grouped = staging.tile([P, PACK * BANK], BF16, name="us_grouped", tag="grouped", align_bytes=64)
+            for half in range(2):
+                bank = transpose_words([words[:, 256 * (2 * half + j) : 256 * (2 * half + j + 1)] for j in range(2)])
+                nc.vector.tensor_tensor(
+                    out=grouped[:, 1024 * half : 1024 * (half + 1)].rearrange("p (c u e) -> p c u e", u=2, e=2),
+                    in0=bank[:].bitcast(BF16).rearrange("p (u c e) -> p c u e", u=2, e=2),
+                    in1=s_grid[:].unsqueeze(1).to_broadcast([P, 256, 2, 2]),
+                    op=ALU.mult,
+                )
+            quantise_later(slot, grouped[:], us_codes[g][:], us_scales[g][:])
+
+        def prepare_v(slot, c):
+            words = v_raw[c][:].bitcast(F32)
+            grouped = staging.tile([P, PACK * CHUNK], BF16, name="v_grouped", tag="grouped", align_bytes=64)
+            for half in range(2):
+                bank = transpose_words([words[:, 256 * (2 * half + j) : 256 * (2 * half + j + 1)] for j in range(2)])
+                copy = nc.scalar.copy if c == 0 else nc.vector.tensor_copy
+                copy_words_out(copy, grouped[:, 1024 * half : 1024 * (half + 1)], bank)
+            quantise_later(slot, grouped[:], v_codes[c][:], v_scales[c][:])
+
+        def prepare_x(slot):
+            for g in range(D_PASSES):
+                grouped = staging.tile([P, PACK * BANK], BF16, name="x_grouped", tag="grouped", align_bytes=64)
+                for pair in range(BATCH // 2):
+                    words = x_raw[pair][:].bitcast(F32)
+                    bank = transpose_words([words[:, 512 * j + 256 * g : 512 * j + 256 * (g + 1)] for j in range(2)])
+                    copy_words_out(nc.scalar.copy, grouped[:, 1024 * pair : 1024 * (pair + 1)], bank)
+                quantise_later(slot, grouped[:], x_codes[g][:], x_scales[g][:])
+
+        def build_w(slot):
+            c, k = divmod(slot, SLOTS_PER_CHUNK)
+            g, half = divmod(k, 2)
+            if k == 0:
+                w_codes[c] = w_pool.tile([P, D_PASSES * CHUNK], U32, name="w_codes", align_bytes=64)
+                w_scales[c] = w_pool.tile([P, D_PASSES * CHUNK], U8, name="w_scales", align_bytes=64)
+            grouped = staging.tile([P, PACK * 256], BF16, name="w_grouped", bufs=4, align_bytes=64)
+            for j in range(2):
+                cols = slice(P * (2 * half + j), P * (2 * half + j + 1))
+                bank = psum.tile([P, BANK], F32, name="bank", tag="bank")
+                for t in range(PACK):
+                    nc.tensor.matmul_mx(
+                        out=bank[:, P * t : P * (t + 1)],
+                        lhsT=us_codes[g][:, P * t : P * (t + 1)].bitcast(FP8X4),
+                        lhsT_scale=us_scales[g][:, P * t : P * (t + 1)],
+                        rhs=v_codes[c][:, cols].bitcast(FP8X4),
+                        rhs_scale=v_scales[c][:, cols],
+                        start=True,
+                        stop=True,
+                    )
+                copy = nc.vector.tensor_copy if (k == VECTOR_W_SLOT and j == 0) else nc.scalar.copy
+                copy(
+                    out=grouped[:, BANK * j : BANK * (j + 1)].rearrange("p (f t) -> p f t", t=PACK),
+                    in_=bank[:].rearrange("p (t f) -> p f t", t=PACK),
+                )
+            first = CHUNK * g + 256 * half
+            quantise_later(slot, grouped[:], w_codes[c][:, first : first + 256], w_scales[c][:, first : first + 256])
+
+        def apply_w(c, b):
+            bank = psum.tile([P, BANK], F32, name="bank", tag="bank")
+            for g in range(D_PASSES):
+                nc.tensor.matmul_mx(
+                    out=bank[:],
+                    lhsT=x_codes[g][:, P * b : P * (b + 1)].bitcast(FP8X4),
+                    lhsT_scale=x_scales[g][:, P * b : P * (b + 1)],
+                    rhs=w_codes[c][:, CHUNK * g : CHUNK * (g + 1)].bitcast(FP8X4),
+                    rhs_scale=w_scales[c][:, CHUNK * g : CHUNK * (g + 1)],
+                    start=(g == 0),
+                    stop=(g == D_PASSES - 1),
+                )
+            h_sb = h_pool.tile([P, CHUNK], F32, name="h_sb")
+            nc.vector.tensor_tensor(
+                out=h_sb[:], in0=bank[:], in1=bias_all[:, CHUNK * c : CHUNK * (c + 1)], op=ALU.add
+            )
+            return h_sb
+
+        def gelu_and_store(c, b, h_sb):
+            nc.scalar.activation(out=h_sb[:], in_=h_sb[:], func=ACT.Gelu)
+            nc.sync.dma_start(out=out[b, :, CHUNK * c : CHUNK * (c + 1)], in_=h_sb[:])
+
+        prepare_us(-1, 0)
+        prepare_v(-1, 0)
+        biased = {}
+        for slot in range(W_SLOTS + LAG + 1):
+            quantise_what_waits(slot - 1)
+            if slot < W_SLOTS:
+                build_w(slot)
+            if 0 <= slot - LAG < W_SLOTS:
+                c, b = divmod(slot - LAG, BATCH)
+                biased[slot] = (c, b, apply_w(c, b))
+            if slot - 1 in biased:
+                c, b, h_sb = biased[slot - 1]
+                gelu_and_store(c, b, h_sb)
+            if slot == 0:
+                prepare_us(slot, 1)
+            if slot == X_SLOT:
+                prepare_x(slot)
+            next_chunk = slot // SLOTS_PER_CHUNK + 1
+            if slot % SLOTS_PER_CHUNK == 0 and next_chunk < N_CHUNKS:
+                prepare_v(slot, next_chunk)

@@ -20,7 +20,8 @@ N_CHUNKS = DFF // CHUNK
 D_PASSES = D // (P * PACK)
 SLOTS_PER_CHUNK = 4
 W_SLOTS = N_CHUNKS * SLOTS_PER_CHUNK
-LAG = 5
+LAG = 6
+GELU_LAG = 2
 X_SLOT = 2
 VECTOR_W_SLOT = 2
 
@@ -35,21 +36,24 @@ def tile_hybridsuperlayer_pa_kernel(tc, x, c_fc_U, c_fc_S, c_fc_V, c_fc_bias, ou
         w_pool = ctx.enter_context(tc.tile_pool(name="w_pool", bufs=3))
         h_pool = ctx.enter_context(tc.tile_pool(name="h_pool", bufs=6))
         psum = ctx.enter_context(tc.psum_pool(name="psum", bufs=8))
+        ctx.enter_context(tc.manual_schedule())
 
         s_grid = resident.tile([P, 2, 2], BF16, name="s_grid")
-        nc.sync.dma_start(out=s_grid[:], in_=c_fc_S.rearrange("(u p e) -> p u e", u=2, p=P, e=2))
+        nc.scalar.dma_start(out=s_grid[:], in_=c_fc_S.rearrange("(u p e) -> p u e", u=2, p=P, e=2))
 
-        u_rows = c_fc_U.rearrange("(g u m e) r -> g m u e r", g=D_PASSES, u=2, m=P, e=2)
-        u_raw = [resident.tile([P, PACK * R], BF16, name="u_raw%d" % g) for g in range(D_PASSES)]
+        u_rows = c_fc_U.rearrange("(g u m e) r -> g u m e r", g=D_PASSES, u=2, m=P, e=2)
+        u_raw = [
+            [resident.tile([P, 2 * R], BF16, name="u_raw%d%d" % (g, u)) for u in range(2)]
+            for g in range(D_PASSES)
+        ]
         v_rows = c_fc_V.rearrange("(c a p) r -> c p a r", c=N_CHUNKS, a=CHUNK // P, p=P)
         v_raw = [resident.tile([P, CHUNK // P * R], BF16, name="v_raw%d" % c) for c in range(N_CHUNKS)]
         x_raw = [resident.tile([P, 2 * D], BF16, name="x_raw%d" % pair) for pair in range(BATCH // 2)]
         bias_all = resident.tile([P, DFF], BF16, name="bias_all")
 
         def load_u(g):
-            nc.sync.dma_start(
-                out=u_raw[g][:].rearrange("m (u e r) -> m u e r", u=2, e=2), in_=u_rows[g]
-            )
+            for u in range(2):
+                nc.sync.dma_start(out=u_raw[g][u][:].rearrange("m (e r) -> m e r", e=2), in_=u_rows[g, u])
 
         def load_v(c):
             nc.sync.dma_start(out=v_raw[c][:].rearrange("p (a r) -> p a r", r=R), in_=v_rows[c])
@@ -111,10 +115,10 @@ def tile_hybridsuperlayer_pa_kernel(tc, x, c_fc_U, c_fc_S, c_fc_V, c_fc_bias, ou
             )
 
         def prepare_us(slot, g):
-            words = u_raw[g][:].bitcast(F32)
             grouped = staging.tile([P, PACK * BANK], BF16, name="us_grouped", tag="grouped", align_bytes=64)
             for half in range(2):
-                bank = transpose_words([words[:, 256 * (2 * half + j) : 256 * (2 * half + j + 1)] for j in range(2)])
+                words = u_raw[g][half][:].bitcast(F32)
+                bank = transpose_words([words[:, 256 * j : 256 * (j + 1)] for j in range(2)])
                 nc.vector.tensor_tensor(
                     out=grouped[:, 1024 * half : 1024 * (half + 1)].rearrange("p (c u e) -> p c u e", u=2, e=2),
                     in0=bank[:].bitcast(BF16).rearrange("p (u c e) -> p c u e", u=2, e=2),
@@ -194,16 +198,8 @@ def tile_hybridsuperlayer_pa_kernel(tc, x, c_fc_U, c_fc_S, c_fc_V, c_fc_bias, ou
         prepare_us(-1, 0)
         prepare_v(-1, 0)
         biased = {}
-        for slot in range(W_SLOTS + LAG + 1):
+        for slot in range(W_SLOTS + LAG + GELU_LAG):
             quantise_what_waits(slot - 1)
-            if slot < W_SLOTS:
-                build_w(slot)
-            if 0 <= slot - LAG < W_SLOTS:
-                c, b = divmod(slot - LAG, BATCH)
-                biased[slot] = (c, b, apply_w(c, b))
-            if slot - 1 in biased:
-                c, b, h_sb = biased[slot - 1]
-                gelu_and_store(c, b, h_sb)
             if slot == 0:
                 prepare_us(slot, 1)
             if slot == X_SLOT:
@@ -211,3 +207,11 @@ def tile_hybridsuperlayer_pa_kernel(tc, x, c_fc_U, c_fc_S, c_fc_V, c_fc_bias, ou
             next_chunk = slot // SLOTS_PER_CHUNK + 1
             if slot % SLOTS_PER_CHUNK == 0 and next_chunk < N_CHUNKS:
                 prepare_v(slot, next_chunk)
+            if slot < W_SLOTS:
+                build_w(slot)
+            if 0 <= slot - LAG < W_SLOTS:
+                c, b = divmod(slot - LAG, BATCH)
+                biased[slot] = (c, b, apply_w(c, b))
+            if slot - GELU_LAG in biased:
+                c, b, h_sb = biased[slot - GELU_LAG]
+                gelu_and_store(c, b, h_sb)

@@ -23,7 +23,7 @@ W_SLOTS = N_CHUNKS * SLOTS_PER_CHUNK
 LAG = 6
 GELU_LAG = 2
 X_SLOT = 2
-VECTOR_W_SLOT = 2
+VECTOR_SHARE = 6
 
 FLOPS = 2 * D * DFF * R + 2 * BATCH * SEQ * D * DFF
 
@@ -165,7 +165,7 @@ def tile_hybridsuperlayer_pa_kernel(tc, x, c_fc_U, c_fc_S, c_fc_V, c_fc_bias, ou
                         start=True,
                         stop=True,
                     )
-                copy = nc.vector.tensor_copy if (k == VECTOR_W_SLOT and j == 0) else nc.scalar.copy
+                copy = nc.vector.tensor_copy if (2 * slot + j) % VECTOR_SHARE == VECTOR_SHARE - 1 else nc.scalar.copy
                 copy(
                     out=grouped[:, BANK * j : BANK * (j + 1)].rearrange("p (f t) -> p f t", t=PACK),
                     in_=bank[:].rearrange("p (t f) -> p f t", t=PACK),

@@ -20,9 +20,9 @@ N_CHUNKS = DFF // CHUNK
 D_PASSES = D // (P * PACK)
 SLOTS_PER_CHUNK = 4
 W_SLOTS = N_CHUNKS * SLOTS_PER_CHUNK
-LAG = 6
+LAG = 8
 GELU_LAG = 2
-X_SLOT = 2
+X_SLOT = 3
 VECTOR_SHARE = 6
 
 FLOPS = 2 * D * DFF * R + 2 * BATCH * SEQ * D * DFF
@@ -33,8 +33,8 @@ def tile_hybridsuperlayer_pa_kernel(tc, x, c_fc_U, c_fc_S, c_fc_V, c_fc_bias, ou
     with ExitStack() as ctx:
         resident = ctx.enter_context(tc.tile_pool(name="resident", bufs=1))
         staging = ctx.enter_context(tc.tile_pool(name="staging", bufs=3))
-        w_pool = ctx.enter_context(tc.tile_pool(name="w_pool", bufs=3))
-        h_pool = ctx.enter_context(tc.tile_pool(name="h_pool", bufs=6))
+        w_pool = ctx.enter_context(tc.tile_pool(name="w_pool", bufs=4))
+        h_pool = ctx.enter_context(tc.tile_pool(name="h_pool", bufs=12))
         psum = ctx.enter_context(tc.psum_pool(name="psum", bufs=8))
         ctx.enter_context(tc.manual_schedule())
 
@@ -151,7 +151,7 @@ def tile_hybridsuperlayer_pa_kernel(tc, x, c_fc_U, c_fc_S, c_fc_V, c_fc_bias, ou
             if k == 0:
                 w_codes[c] = w_pool.tile([P, D_PASSES * CHUNK], U32, name="w_codes", align_bytes=64)
                 w_scales[c] = w_pool.tile([P, D_PASSES * CHUNK], U8, name="w_scales", align_bytes=64)
-            grouped = staging.tile([P, PACK * 256], BF16, name="w_grouped", bufs=4, align_bytes=64)
+            grouped = staging.tile([P, PACK * 256], BF16, name="w_grouped", bufs=6, align_bytes=64)
             for j in range(2):
                 cols = slice(P * (2 * half + j), P * (2 * half + j + 1))
                 bank = psum.tile([P, BANK], F32, name="bank", tag="bank")
@@ -171,7 +171,7 @@ def tile_hybridsuperlayer_pa_kernel(tc, x, c_fc_U, c_fc_S, c_fc_V, c_fc_bias, ou
                     in_=bank[:].rearrange("p (t f) -> p f t", t=PACK),
                 )
             first = CHUNK * g + 256 * half
-            quantise_later(slot, grouped[:], w_codes[c][:, first : first + 256], w_scales[c][:, first : first + 256])
+            quantise_later(slot + 1, grouped[:], w_codes[c][:, first : first + 256], w_scales[c][:, first : first + 256])
 
         def apply_w(c, b):
             bank = psum.tile([P, BANK], F32, name="bank", tag="bank")
@@ -205,7 +205,9 @@ def tile_hybridsuperlayer_pa_kernel(tc, x, c_fc_U, c_fc_S, c_fc_V, c_fc_bias, ou
             if slot == X_SLOT:
                 prepare_x(slot)
             next_chunk = slot // SLOTS_PER_CHUNK + 1
-            if slot % SLOTS_PER_CHUNK == 0 and next_chunk < N_CHUNKS:
+            if slot == 1:
+                prepare_v(slot, 1)
+            if slot % SLOTS_PER_CHUNK == 0 and 1 < next_chunk < N_CHUNKS:
                 prepare_v(slot, next_chunk)
             if slot < W_SLOTS:
                 build_w(slot)

from contextlib import ExitStack

import concourse.mybir as mybir
from concourse.masks import make_identity

F32 = mybir.dt.float32
BF16 = mybir.dt.bfloat16
U32 = mybir.dt.uint32
U8 = mybir.dt.uint8
FP8X4 = mybir.dt.float8_e4m3fn_x4
ALU = mybir.AluOpType
ACT = mybir.ActivationFunctionType

P = 128
PACK = 4
BATCH, SEQ, D, DFF, R = 4, 128, 1024, 4096, 512
BANK = 512
CHUNK = 512
N_CHUNKS = DFF // CHUNK
D_PASSES = D // (P * PACK)
SLOTS_PER_CHUNK = 4
W_SLOTS = N_CHUNKS * SLOTS_PER_CHUNK
LAG = 8
GELU_LAG = 2
X_SLOT = 3
VECTOR_SHARE = 6

FLOPS = 2 * D * DFF * R + 2 * BATCH * SEQ * D * DFF


def tile_hybridsuperlayer_pa_kernel(tc, x, c_fc_U, c_fc_S, c_fc_V, c_fc_bias, out):
    nc = tc.nc
    with ExitStack() as ctx:
        resident = ctx.enter_context(tc.tile_pool(name="resident", bufs=1))
        staging = ctx.enter_context(tc.tile_pool(name="staging", bufs=3))
        w_pool = ctx.enter_context(tc.tile_pool(name="w_pool", bufs=4))
        h_pool = ctx.enter_context(tc.tile_pool(name="h_pool", bufs=12))
        psum = ctx.enter_context(tc.psum_pool(name="psum", bufs=8))
        ctx.enter_context(tc.manual_schedule())

        s_grid = resident.tile([P, 2, 2], BF16, name="s_grid")
        nc.scalar.dma_start(out=s_grid[:], in_=c_fc_S.rearrange("(u p e) -> p u e", u=2, p=P, e=2))

        u_rows = c_fc_U.rearrange("(g u m e) r -> g u m e r", g=D_PASSES, u=2, m=P, e=2)
        u_raw = [
            [resident.tile([P, 2 * R], BF16, name="u_raw%d%d" % (g, u)) for u in range(2)]
            for g in range(D_PASSES)
        ]
        v_rows = c_fc_V.rearrange("(c a p) r -> c p a r", c=N_CHUNKS, a=CHUNK // P, p=P)
        v_raw = [resident.tile([P, CHUNK // P * R], BF16, name="v_raw%d" % c) for c in range(N_CHUNKS)]
        x_raw = [resident.tile([P, 2 * D], BF16, name="x_raw%d" % pair) for pair in range(BATCH // 2)]
        bias_all = resident.tile([P, DFF], BF16, name="bias_all")

        def load_u(g):
            for u in range(2):
                nc.sync.dma_start(out=u_raw[g][u][:].rearrange("m (e r) -> m e r", e=2), in_=u_rows[g, u])

        def load_v(c):
            nc.sync.dma_start(out=v_raw[c][:].rearrange("p (a r) -> p a r", r=R), in_=v_rows[c])

        load_u(0)
        load_v(0)
        load_u(1)
        load_v(1)
        for pair in range(BATCH // 2):
            nc.sync.dma_start(
                out=x_raw[pair][:].rearrange("s (j d) -> s j d", j=2),
                in_=x[2 * pair : 2 * pair + 2].rearrange("j s d -> s j d"),
            )
        load_v(2)
        nc.sync.dma_start(out=bias_all[:], in_=c_fc_bias.partition_broadcast(P))
        for c in range(3, N_CHUNKS):
            load_v(c)

        identity = resident.tile([P, P], F32, name="identity")
        make_identity(nc, identity[:])

        table_warmer = resident.tile([P, 1], F32, name="table_warmer")
        nc.vector.memset(table_warmer[:], 0.0)
        nc.scalar.activation(out=table_warmer[:], in_=table_warmer[:], func=ACT.Gelu)

        us_codes = [resident.tile([P, BANK], U32, name="us_codes%d" % g, align_bytes=64) for g in range(D_PASSES)]
        us_scales = [resident.tile([P, BANK], U8, name="us_scales%d" % g, align_bytes=64) for g in range(D_PASSES)]
        x_codes = [resident.tile([P, BANK], U32, name="x_codes%d" % g, align_bytes=64) for g in range(D_PASSES)]
        x_scales = [resident.tile([P, BANK], U8, name="x_scales%d" % g, align_bytes=64) for g in range(D_PASSES)]
        v_codes = [resident.tile([P, CHUNK], U32, name="v_codes%d" % c, align_bytes=64) for c in range(N_CHUNKS)]
        v_scales = [resident.tile([P, CHUNK], U8, name="v_scales%d" % c, align_bytes=64) for c in range(N_CHUNKS)]
        w_codes = {}
        w_scales = {}

        waiting = {}

        def quantise_later(slot, grouped, codes, scales):
            waiting[slot] = waiting.get(slot, []) + [(grouped, codes, scales)]

        def quantise_what_waits(slot):
            for grouped, codes, scales in waiting.get(slot, []):
                nc.vector.quantize_mx(out=codes.bitcast(FP8X4), scales=scales, in_=grouped)

        def transpose_words(row_tiles):
            bank = psum.tile([P, BANK], F32, name="bank", tag="bank")
            for j in range(2):
                for u in range(2):
                    nc.tensor.transpose(
                        bank[:, 256 * u + P * j : 256 * u + P * j + P],
                        row_tiles[j][:, P * u : P * u + P],
                        identity[:],
                    )
            return bank

        def copy_words_out(copy, grouped_half, bank):
            copy(
                out=grouped_half.bitcast(F32).rearrange("p (c u) -> p c u", u=2),
                in_=bank[:].rearrange("p (u c) -> p c u", u=2),
            )

        def prepare_us(slot, g):
            grouped = staging.tile([P, PACK * BANK], BF16, name="us_grouped", tag="grouped", align_bytes=64)
            for half in range(2):
                words = u_raw[g][half][:].bitcast(F32)
                bank = transpose_words([words[:, 256 * j : 256 * (j + 1)] for j in range(2)])
                nc.vector.tensor_tensor(
                    out=grouped[:, 1024 * half : 1024 * (half + 1)].rearrange("p (c u e) -> p c u e", u=2, e=2),
                    in0=bank[:].bitcast(BF16).rearrange("p (u c e) -> p c u e", u=2, e=2),
                    in1=s_grid[:].unsqueeze(1).to_broadcast([P, 256, 2, 2]),
                    op=ALU.mult,
                )
            quantise_later(slot, grouped[:], us_codes[g][:], us_scales[g][:])

        def prepare_v(slot, c):
            words = v_raw[c][:].bitcast(F32)
            grouped = staging.tile([P, PACK * CHUNK], BF16, name="v_grouped", tag="grouped", align_bytes=64)
            for half in range(2):
                bank = transpose_words([words[:, 256 * (2 * half + j) : 256 * (2 * half + j + 1)] for j in range(2)])
                copy = nc.scalar.copy if c == 0 else nc.vector.tensor_copy
                copy_words_out(copy, grouped[:, 1024 * half : 1024 * (half + 1)], bank)
            quantise_later(slot, grouped[:], v_codes[c][:], v_scales[c][:])

        def prepare_x(slot):
            for g in range(D_PASSES):
                grouped = staging.tile([P, PACK * BANK], BF16, name="x_grouped", tag="grouped", align_bytes=64)
                for pair in range(BATCH // 2):
                    words = x_raw[pair][:].bitcast(F32)
                    bank = transpose_words([words[:, 512 * j + 256 * g : 512 * j + 256 * (g + 1)] for j in range(2)])
                    copy_words_out(nc.scalar.copy, grouped[:, 1024 * pair : 1024 * (pair + 1)], bank)
                quantise_later(slot, grouped[:], x_codes[g][:], x_scales[g][:])

        def build_w(slot):
            c, k = divmod(slot, SLOTS_PER_CHUNK)
            g, half = divmod(k, 2)
            if k == 0:
                w_codes[c] = w_pool.tile([P, D_PASSES * CHUNK], U32, name="w_codes", align_bytes=64)
                w_scales[c] = w_pool.tile([P, D_PASSES * CHUNK], U8, name="w_scales", align_bytes=64)
            grouped = staging.tile([P, PACK * 256], BF16, name="w_grouped", bufs=6, align_bytes=64)
            for j in range(2):
                cols = slice(P * (2 * half + j), P * (2 * half + j + 1))
                bank = psum.tile([P, BANK], F32, name="bank", tag="bank")
                for t in range(PACK):
                    nc.tensor.matmul_mx(
                        out=bank[:, P * t : P * (t + 1)],
                        lhsT=us_codes[g][:, P * t : P * (t + 1)].bitcast(FP8X4),
                        lhsT_scale=us_scales[g][:, P * t : P * (t + 1)],
                        rhs=v_codes[c][:, cols].bitcast(FP8X4),
                        rhs_scale=v_scales[c][:, cols],
                        start=True,
                        stop=True,
                    )
                copy = nc.vector.tensor_copy if (2 * slot + j) % VECTOR_SHARE == VECTOR_SHARE - 1 else nc.scalar.copy
                copy(
                    out=grouped[:, BANK * j : BANK * (j + 1)].rearrange("p (f t) -> p f t", t=PACK),
                    in_=bank[:].rearrange("p (t f) -> p f t", t=PACK),
                )
            first = CHUNK * g + 256 * half
            quantise_later(slot + 1, grouped[:], w_codes[c][:, first : first + 256], w_scales[c][:, first : first + 256])

        def apply_w(c, b):
            bank = psum.tile([P, BANK], F32, name="bank", tag="bank")
            for g in range(D_PASSES):
                nc.tensor.matmul_mx(
                    out=bank[:],
                    lhsT=x_codes[g][:, P * b : P * (b + 1)].bitcast(FP8X4),
                    lhsT_scale=x_scales[g][:, P * b : P * (b + 1)],
                    rhs=w_codes[c][:, CHUNK * g : CHUNK * (g + 1)].bitcast(FP8X4),
                    rhs_scale=w_scales[c][:, CHUNK * g : CHUNK * (g + 1)],
                    start=(g == 0),
                    stop=(g == D_PASSES - 1),
                )
            h_sb = h_pool.tile([P, CHUNK], F32, name="h_sb")
            nc.vector.tensor_tensor(
                out=h_sb[:], in0=bank[:], in1=bias_all[:, CHUNK * c : CHUNK * (c + 1)], op=ALU.add
            )
            return h_sb

        def gelu_and_store(c, b, h_sb):
            nc.scalar.activation(out=h_sb[:], in_=h_sb[:], func=ACT.Gelu)
            nc.sync.dma_start(out=out[b, :, CHUNK * c : CHUNK * (c + 1)], in_=h_sb[:])

        prepare_us(-1, 0)
        prepare_v(-1, 0)
        biased = {}
        for slot in range(W_SLOTS + LAG + GELU_LAG):
            quantise_what_waits(slot - 1)
            if slot == 0:
                prepare_us(slot, 1)
            if slot == X_SLOT:
                prepare_x(slot)
            next_chunk = slot // SLOTS_PER_CHUNK + 1
            if slot == 1:
                prepare_v(slot, 1)
            if slot % SLOTS_PER_CHUNK == 0 and 1 < next_chunk < N_CHUNKS:
                prepare_v(slot, next_chunk)
            if slot < W_SLOTS:
                build_w(slot)
            if 0 <= slot - LAG < W_SLOTS:
                c, b = divmod(slot - LAG, BATCH)
                biased[slot] = (c, b, apply_w(c, b))
            if slot - GELU_LAG in biased:
                c, b, h_sb = biased[slot - GELU_LAG]
                gelu_and_store(c, b, h_sb)
